import numpy as np
import ml_dtypes


def mxq(x, axis, fmt="e4m3"):
    dtype, down = {"e4m3": (ml_dtypes.float8_e4m3fn, 7), "e5m2": (ml_dtypes.float8_e5m2, 14)}[fmt]
    v = np.moveaxis(np.asarray(x, np.float32).astype(ml_dtypes.bfloat16).astype(np.float64), axis, -1)
    blocks = v.reshape(v.shape[:-1] + (-1, 32))
    amax = np.abs(blocks).max(-1, keepdims=True)
    byte = np.maximum(np.where(amax > 0, np.frexp(amax)[1] - 1 + 127, 0) - down, 1)
    scale = np.exp2(byte - 127.0)
    codes = (blocks / scale).astype(np.float32).astype(dtype).astype(np.float64)
    return np.moveaxis((codes * scale).reshape(v.shape), -1, axis)


WIDE = False


def mx_kscale(k):
    if not WIDE:
        return np.ones(k)
    levels = np.array([10, -10, 5, -5, 0])
    if k % 512:
        return np.exp2(np.random.permutation(np.resize(levels, k // 32))).repeat(32)
    a = np.empty((k // 512, 16))
    for p in range(k // 512):
        a[p, :8] = np.random.permutation(np.resize(levels, 8))
        for g in range(8):
            far = levels[np.abs(levels - a[p, g]) >= 10]
            a[p, g + 8] = far[np.random.randint(len(far))]
    return np.exp2(a.ravel()).repeat(32)


BF16 = ml_dtypes.bfloat16


def bf(x):
    return np.asarray(x, np.float32).astype(BF16)


def f64(x):
    return np.asarray(x).astype(np.float64)


B, S, H, NH, FF = 2, 512, 1024, 8, 3072
HD = H // NH
EPS = 1e-7


def layer_norm(x, g, b):
    m = x.mean(-1, keepdims=True)
    v = ((x - m) ** 2).mean(-1, keepdims=True)
    return (x - m) / np.sqrt(v + EPS) * g + b


def heads(t):
    return t.reshape(B, S, NH, HD).transpose(0, 2, 1, 3)


def setup_inputs():
    s = mx_kscale(H)
    r = np.random.standard_normal
    return {"x": bf(r((B, S, H))), "pos_emb": bf(r((S, H)) * 0.5),
            "emb_ln_g": bf((1.0 + 0.1 * r(H)) * s), "emb_ln_b": bf(0.1 * r(H) * s),
            "Wq": bf(r((H, H)) * 1.5 / np.sqrt(H) / s[:, None]),
            "Wk": bf(r((H, H)) * 1.5 / np.sqrt(H) / s[:, None]),
            "Wv": bf(r((H, H)) * 2.0 / np.sqrt(H) / s[:, None]),
            "q_bias": bf(r(H) * 0.3), "v_bias": bf(r(H) * 0.3)}


def reference(x, pos_emb, emb_ln_g, emb_ln_b, Wq, Wk, Wv, q_bias, v_bias):
    h = layer_norm(f64(x) + f64(pos_emb), f64(emb_ln_g), f64(emb_ln_b))
    hq = mxq(h, 2, "e4m3")
    q = heads((hq @ mxq(f64(Wq), 0, "e4m3")) + f64(q_bias))
    k = heads(hq @ mxq(f64(Wk), 0, "e4m3"))
    v = heads((hq @ mxq(f64(Wv), 0, "e4m3")) + f64(v_bias))
    return q / np.sqrt(HD), k, v

@@ -1,0 +1,316 @@
+from contextlib import ExitStack
+import math
+
+import concourse.mybir as mybir
+from concourse.masks import make_identity
+
+F32 = mybir.dt.float32
+BF16 = mybir.dt.bfloat16
+U32 = mybir.dt.uint32
+U8 = mybir.dt.uint8
+FP8X4 = mybir.dt.float8_e4m3fn_x4
+ALU = mybir.AluOpType
+ACT = mybir.ActivationFunctionType
+
+P = 128
+PACK = 4
+B = 2
+S = 512
+H = 1024
+HD = 128
+EPS = 1e-7
+PASSES = H // (P * PACK)
+TOK_TILES = S // P
+N_TILES = B * TOK_TILES
+ROUNDS = B * PASSES
+BANK = 512
+CHUNK = BANK
+CHUNK_HEADS = CHUNK // HD
+K_TILES = H // P
+CHUNKS = [(0, 0), (0, 1), (1, 0), (2, 0), (1, 1), (2, 1)]
+PIECES = len(CHUNKS) * PASSES
+UNITS = len(CHUNKS) * B
+AHEAD = 4
+
+FLOPS = 2 * B * S * H * 3 * H
+
+
+def tile_disentangledattention_pa_kernel(
+    tc, x, pos_emb, emb_ln_g, emb_ln_b, Wq, Wk, Wv, q_bias, v_bias, out_0, out_1, out_2
+):
+    nc = tc.nc
+    weights = [Wq, Wk, Wv]
+    outs = [out_0, out_1, out_2]
+    inv_sqrt_hd = 1.0 / math.sqrt(HD)
+
+    with ExitStack() as ctx:
+        keep = ctx.enter_context(tc.tile_pool(name="keep", bufs=1))
+        tokens = ctx.enter_context(tc.tile_pool(name="tokens", bufs=N_TILES))
+        stats = ctx.enter_context(tc.tile_pool(name="stats", bufs=4))
+        work = ctx.enter_context(tc.tile_pool(name="work", bufs=2))
+        pieces = ctx.enter_context(tc.tile_pool(name="pieces", bufs=4))
+        stores = ctx.enter_context(tc.tile_pool(name="stores", bufs=4))
+        psum = ctx.enter_context(tc.psum_pool(name="psum", bufs=8))
+        ctx.enter_context(tc.manual_schedule())
+
+        ident_bf16 = keep.tile([P, P], BF16)
+        make_identity(nc, ident_bf16[:])
+        ident_f32 = keep.tile([P, P], F32)
+        make_identity(nc, ident_f32[:])
+        minus_half = keep.tile([P, 1], F32)
+        nc.gpsimd.memset(minus_half[:], -0.5)
+
+        x_sb = keep.tile([P, B, TOK_TILES, H], BF16)
+        pos_sb = keep.tile([P, TOK_TILES, H], BF16)
+        pos_view = pos_emb.rearrange("(p j) h -> p j h", j=TOK_TILES)
+        x_views = [x[b].rearrange("(p j) h -> p j h", j=TOK_TILES) for b in range(B)]
+        for j in range(TOK_TILES):
+            nc.sync.dma_start(out=pos_sb[:, j, :], in_=pos_view[:, j, :])
+            nc.sync.dma_start(out=x_sb[:, 0, j, :], in_=x_views[0][:, j, :])
+        for js in (slice(0, 2), slice(2, 4)):
+            nc.sync.dma_start(out=x_sb[:, 1, js, :], in_=x_views[1][:, js, :])
+        w_raw = [keep.tile([P, PASSES, PACK, H], BF16, name="w_raw%d" % m) for m in range(3)]
+        for m in range(3):
+            w_view = weights[m].rearrange("(c p t) n -> c p t n", c=PASSES, t=PACK)
+            for c in range(PASSES):
+                nc.sync.dma_start(out=w_raw[m][:, c, :, :], in_=w_view[c])
+        bias_bf16 = keep.tile([P, 2, H], BF16)
+        nc.sync.dma_start(out=bias_bf16[:, 0, :], in_=q_bias.partition_broadcast(P))
+        nc.sync.dma_start(out=bias_bf16[:, 1, :], in_=v_bias.partition_broadcast(P))
+        gb_bf16 = []
+        for i, vec in enumerate((emb_ln_g, emb_ln_b)):
+            vec_cols = keep.tile([P, PASSES, PACK], BF16, name="vec_cols%d" % i)
+            nc.scalar.dma_start(
+                out=vec_cols[:], in_=vec.rearrange("(c p t) -> p c t", c=PASSES, t=PACK)
+            )
+            gb_bf16.append(vec_cols)
+
+        h_codes = keep.tile([P, ROUNDS, S], U32, align_bytes=64)
+        h_scales = keep.tile([P, ROUNDS, S], U8, align_bytes=64)
+        w_codes = keep.tile([P, PIECES, CHUNK], U32, align_bytes=64)
+        w_scales = keep.tile([P, PIECES, CHUNK], U8, align_bytes=64)
+
+        def regroup(engine_copy, grouped, planes):
+            engine_copy(
+                out=grouped.rearrange("p (w i) t -> p w t i", i=4),
+                in_=planes.rearrange("p t (w i) -> p w t i", i=4),
+            )
+
+        u_banks = {}
+        moments = {}
+        scale_shift = {}
+        z_toks = {}
+
+        def add_tokens(i):
+            b, j = divmod(i, TOK_TILES)
+            u_banks[i] = []
+            for c in range(PASSES):
+                cols = slice(c * BANK, (c + 1) * BANK)
+                u_bank = psum.tile([P, BANK], F32, tag="bank")
+                nc.tensor.matmul(
+                    u_bank[:], lhsT=ident_bf16[:], rhs=x_sb[:, b, j, cols], start=True, stop=False
+                )
+                nc.tensor.matmul(
+                    u_bank[:], lhsT=ident_bf16[:], rhs=pos_sb[:, j, cols], start=False, stop=True
+                )
+                u_banks[i].append(u_bank)
+            moment = stats.tile([P, PASSES, 6], F32)
+            moments[i] = moment
+
+        def stats_half(i, c):
+            nc.vector.bn_stats(out=moments[i][:, c, :], in_=u_banks[i][c][:])
+
+        def finish_stats(i):
+            mean_var = stats.tile([P, 2], F32)
+            nc.vector.bn_aggr(out=mean_var[:], in_=moments[i][:].rearrange("p c s -> p (c s)"))
+            var_eps = stats.tile([P, 1], F32)
+            nc.gpsimd.tensor_scalar(
+                out=var_eps[:], in0=mean_var[:, 1:2], scalar1=1.0, scalar2=EPS,
+                op0=ALU.mult, op1=ALU.add,
+            )
+            rstd = stats.tile([P, 1], F32)
+            nc.gpsimd.tensor_tensor(out=rstd[:], in0=var_eps[:], in1=minus_half[:], op=ALU.pow)
+            shift = stats.tile([P, 1], F32)
+            nc.gpsimd.tensor_scalar(
+                out=shift[:], in0=mean_var[:, 0:1], scalar1=rstd[:], scalar2=-1.0,
+                op0=ALU.mult, op1=ALU.mult,
+            )
+            scale_shift[i] = (rstd, shift)
+
+        def normalise(i):
+            rstd, shift = scale_shift[i]
+            z_tok = tokens.tile([P, H], F32)
+            for c in range(PASSES):
+                nc.scalar.activation(
+                    out=z_tok[:, c * BANK : (c + 1) * BANK].rearrange("p (t m) -> p t m", t=PACK),
+                    in_=u_banks[i][c][:].rearrange("p (m t) -> p t m", t=PACK),
+                    func=ACT.Identity, scale=rstd[:], bias=shift[:],
+                )
+            z_toks[i] = z_tok
+
+        add_tokens(0)
+        for i in range(N_TILES + 1):
+            if i + 1 < N_TILES:
+                add_tokens(i + 1)
+            if i < N_TILES:
+                stats_half(i, 0)
+            if i >= 1:
+                finish_stats(i - 1)
+            if i < N_TILES:
+                stats_half(i, 1)
+            if i >= 1:
+                normalise(i - 1)
+
+        gain_bias = keep.tile([P, 2 * K_TILES], F32)
+        for i in range(2):
+            nc.vector.tensor_copy(
+                out=gain_bias[:, i * K_TILES : (i + 1) * K_TILES],
+                in_=gb_bf16[i][:].rearrange("p c t -> p (c t)"),
+            )
+
+        zT_banks = {}
+        h_planes = {}
+        h_grouped = {}
+
+        def transpose_round(r):
+            b, c = divmod(r, PASSES)
+            zT_banks[r] = []
+            for t in range(PACK):
+                kt = c * PACK + t
+                zT_bank = psum.tile([P, S], F32, tag="bank")
+                for j in range(TOK_TILES):
+                    nc.tensor.transpose(
+                        zT_bank[:, j * P : (j + 1) * P],
+                        z_toks[b * TOK_TILES + j][:, kt * P : (kt + 1) * P],
+                        ident_f32[:],
+                    )
+                zT_banks[r].append(zT_bank)
+
+        def scale_round(r):
+            c = r % PASSES
+            planes = work.tile([P, PACK, S], BF16)
+            for t in range(PACK):
+                kt = c * PACK + t
+                gain = gain_bias[:, kt : kt + 1]
+                bias = gain_bias[:, K_TILES + kt : K_TILES + kt + 1]
+                if r == 0:
+                    nc.vector.tensor_scalar(
+                        out=planes[:, t, :], in0=zT_banks[r][t][:], scalar1=gain, scalar2=bias,
+                        op0=ALU.mult, op1=ALU.add,
+                    )
+                else:
+                    nc.scalar.activation(
+                        out=planes[:, t, :], in_=zT_banks[r][t][:], func=ACT.Identity,
+                        scale=gain, bias=bias,
+                    )
+            h_planes[r] = planes
+
+        def regroup_round(r):
+            grouped = work.tile([P, S, PACK], BF16, align_bytes=64)
+            regroup(nc.vector.tensor_copy, grouped[:], h_planes[r][:])
+            h_grouped[r] = grouped
+
+        def quantise_round(r):
+            nc.vector.quantize_mx(
+                out=h_codes[:, r, :].bitcast(FP8X4),
+                scales=h_scales[:, r, :],
+                in_=h_grouped[r][:].rearrange("p w t -> p (w t)"),
+            )
+
+        w_grouped = {}
+
+        def regroup_piece(piece, engine_copy):
+            (m, half), c = CHUNKS[piece // PASSES], piece % PASSES
+            grouped_w = pieces.tile([P, CHUNK, PACK], BF16, align_bytes=64)
+            regroup(engine_copy, grouped_w[:], w_raw[m][:, c, :, half * CHUNK : (half + 1) * CHUNK])
+            w_grouped[piece] = grouped_w
+
+        def quantise_piece(piece):
+            nc.vector.quantize_mx(
+                out=w_codes[:, piece, :].bitcast(FP8X4),
+                scales=w_scales[:, piece, :],
+                in_=w_grouped[piece][:].rearrange("p w t -> p (w t)"),
+            )
+
+        transpose_round(0)
+        transpose_round(1)
+        for r in range(ROUNDS):
+            scale_round(r)
+            if r + 2 < ROUNDS:
+                transpose_round(r + 2)
+            if r >= 1:
+                if r - 1 < PASSES:
+                    quantise_piece(r - 1)
+                quantise_round(r - 1)
+            if r < PASSES:
+                regroup_piece(r, nc.vector.tensor_copy)
+            regroup_round(r)
+        quantise_round(ROUNDS - 1)
+        for piece in range(PASSES, AHEAD):
+            regroup_piece(piece, nc.scalar.copy)
+        quantised = PASSES
+
+        bias_all = keep.tile([P, 2, H], F32)
+        for i, factor in enumerate((inv_sqrt_hd, 1.0)):
+            nc.gpsimd.tensor_scalar(
+                out=bias_all[:, i, :], in0=bias_bf16[:, i, :], scalar1=factor, scalar2=0.0,
+                op0=ALU.mult, op1=ALU.add,
+            )
+
+        acc_banks = {}
+
+        def multiply_unit(n):
+            chunk, b = divmod(n, B)
+            acc_banks[n] = []
+            for j in range(TOK_TILES):
+                acc = psum.tile([P, CHUNK], F32, tag="bank")
+                for c in range(PASSES):
+                    nc.tensor.matmul_mx(
+                        out=acc[:],
+                        lhsT=h_codes[:, b * PASSES + c, j * P : (j + 1) * P].bitcast(FP8X4),
+                        lhsT_scale=h_scales[:, b * PASSES + c, j * P : (j + 1) * P],
+                        rhs=w_codes[:, chunk * PASSES + c, :].bitcast(FP8X4),
+                        rhs_scale=w_scales[:, chunk * PASSES + c, :],
+                        start=(c == 0),
+                        stop=(c == PASSES - 1),
+                    )
+                acc_banks[n].append(acc)
+
+        def empty_unit(n):
+            chunk, b = divmod(n, B)
+            m, half = CHUNKS[chunk]
+            cols = slice(half * CHUNK, (half + 1) * CHUNK)
+            result = stores.tile([P, CHUNK_HEADS, TOK_TILES, HD], F32)
+            for j in range(TOK_TILES):
+                acc_heads = acc_banks[n][j][:].rearrange("p (n d) -> p n d", d=HD)
+                if m == 0:
+                    nc.vector.scalar_tensor_tensor(
+                        out=result[:, :, j, :], in0=acc_heads, scalar=inv_sqrt_hd,
+                        in1=bias_all[:, 0, cols].rearrange("p (n d) -> p n d", d=HD),
+                        op0=ALU.mult, op1=ALU.add,
+                    )
+                elif m == 1:
+                    nc.scalar.copy(out=result[:, :, j, :], in_=acc_heads)
+                else:
+                    nc.vector.tensor_tensor(
+                        out=result[:, :, j, :], in0=acc_heads,
+                        in1=bias_all[:, 1, cols].rearrange("p (n d) -> p n d", d=HD),
+                        op=ALU.add,
+                    )
+            heads = slice(half * CHUNK_HEADS, (half + 1) * CHUNK_HEADS)
+            nc.sync.dma_start(
+                out=outs[m][b, heads].rearrange("n (p j) d -> p n (j d)", j=TOK_TILES),
+                in_=result[:].rearrange("p n j d -> p n (j d)"),
+            )
+
+        multiply_unit(0)
+        for n in range(UNITS):
+            if n + 1 < UNITS:
+                multiply_unit(n + 1)
+            if n + AHEAD < PIECES:
+                unit_of_k = CHUNKS[n // B][0] == 1
+                regroup_piece(n + AHEAD, nc.vector.tensor_copy if unit_of_k else nc.scalar.copy)
+            empty_unit(n)
+            for piece in range(quantised, min(n + AHEAD, PIECES)):
+                quantise_piece(piece)
+            quantised = min(n + AHEAD, PIECES)

@@ -74,9 +74,10 @@ def tile_disentangledattention_pa_kernel(
             w_view = weights[m].rearrange("(c p t) n -> c p t n", c=PASSES, t=PACK)
             for c in range(PASSES):
                 nc.sync.dma_start(out=w_raw[m][:, c, :, :], in_=w_view[c])
-        bias_bf16 = keep.tile([P, 2, H], BF16)
-        nc.sync.dma_start(out=bias_bf16[:, 0, :], in_=q_bias.partition_broadcast(P))
-        nc.sync.dma_start(out=bias_bf16[:, 1, :], in_=v_bias.partition_broadcast(P))
+        bias_rows = keep.tile([P, H], BF16)
+        nc.vector.memset(bias_rows[:], 0.0)
+        for i, vec in enumerate((q_bias, v_bias)):
+            nc.scalar.dma_start(out=bias_rows[i : i + 1, :], in_=vec.rearrange("(r h) -> r h", r=1))
         gb_bf16 = []
         for i, vec in enumerate((emb_ln_g, emb_ln_b)):
             vec_cols = keep.tile([P, PASSES, PACK], BF16, name="vec_cols%d" % i)
@@ -148,10 +149,27 @@ def tile_disentangledattention_pa_kernel(
                 )
             z_toks[i] = z_tok
 
+        bias_all = keep.tile([P, 2, H], F32)
+
+        def spread_bias():
+            for i, factor in enumerate((inv_sqrt_hd, 1.0)):
+                for half in range(PASSES):
+                    cols = slice(half * BANK, (half + 1) * BANK)
+                    bias_bank = psum.tile([P, BANK], F32, tag="bank")
+                    nc.tensor.matmul(
+                        bias_bank[:], lhsT=ident_bf16[:, i : i + 1].to_broadcast([P, P]),
+                        rhs=bias_rows[:, cols], start=True, stop=True,
+                    )
+                    nc.scalar.activation(
+                        out=bias_all[:, i, cols], in_=bias_bank[:], func=ACT.Identity, scale=factor
+                    )
+
         add_tokens(0)
         for i in range(N_TILES + 1):
             if i + 1 < N_TILES:
                 add_tokens(i + 1)
+            if i == 0:
+                spread_bias()
             if i < N_TILES:
                 stats_half(i, 0)
             if i >= 1:
@@ -249,13 +267,6 @@ def tile_disentangledattention_pa_kernel(
         for piece in range(PASSES, AHEAD):
             regroup_piece(piece, nc.scalar.copy)
         quantised = PASSES
-
-        bias_all = keep.tile([P, 2, H], F32)
-        for i, factor in enumerate((inv_sqrt_hd, 1.0)):
-            nc.gpsimd.tensor_scalar(
-                out=bias_all[:, i, :], in0=bias_bf16[:, i, :], scalar1=factor, scalar2=0.0,
-                op0=ALU.mult, op1=ALU.add,
-            )
 
         acc_banks = {}
 

@@ -60,13 +60,19 @@ def tile_disentangledattention_pa_kernel(
         minus_half = keep.tile([P, 1], F32)
         nc.gpsimd.memset(minus_half[:], -0.5)
 
+        bias_rows = keep.tile([P, H], BF16)
+        nc.vector.memset(bias_rows[:].bitcast(U32), 0)
+        for i, vec in enumerate((q_bias, v_bias)):
+            nc.scalar.dma_start(out=bias_rows[i : i + 1, :], in_=vec.rearrange("(r h) -> r h", r=1))
+
         x_sb = keep.tile([P, B, TOK_TILES, H], BF16)
         pos_sb = keep.tile([P, TOK_TILES, H], BF16)
         pos_view = pos_emb.rearrange("(p j) h -> p j h", j=TOK_TILES)
         x_views = [x[b].rearrange("(p j) h -> p j h", j=TOK_TILES) for b in range(B)]
         for j in range(TOK_TILES):
-            nc.sync.dma_start(out=pos_sb[:, j, :], in_=pos_view[:, j, :])
-            nc.sync.dma_start(out=x_sb[:, 0, j, :], in_=x_views[0][:, j, :])
+            for cols in (slice(0, BANK), slice(BANK, H)) if j == 0 else (slice(0, H),):
+                nc.sync.dma_start(out=pos_sb[:, j, cols], in_=pos_view[:, j, cols])
+                nc.sync.dma_start(out=x_sb[:, 0, j, cols], in_=x_views[0][:, j, cols])
         for js in (slice(0, 2), slice(2, 4)):
             nc.sync.dma_start(out=x_sb[:, 1, js, :], in_=x_views[1][:, js, :])
         w_raw = [keep.tile([P, PASSES, PACK, H], BF16, name="w_raw%d" % m) for m in range(3)]
@@ -74,10 +80,6 @@ def tile_disentangledattention_pa_kernel(
             w_view = weights[m].rearrange("(c p t) n -> c p t n", c=PASSES, t=PACK)
             for c in range(PASSES):
                 nc.sync.dma_start(out=w_raw[m][:, c, :, :], in_=w_view[c])
-        bias_rows = keep.tile([P, H], BF16)
-        nc.vector.memset(bias_rows[:], 0.0)
-        for i, vec in enumerate((q_bias, v_bias)):
-            nc.scalar.dma_start(out=bias_rows[i : i + 1, :], in_=vec.rearrange("(r h) -> r h", r=1))
         gb_bf16 = []
         for i, vec in enumerate((emb_ln_g, emb_ln_b)):
             vec_cols = keep.tile([P, PASSES, PACK], BF16, name="vec_cols%d" % i)

@@ -27,7 +27,7 @@ BANK = 512
 CHUNK = BANK
 CHUNK_HEADS = CHUNK // HD
 K_TILES = H // P
-CHUNKS = [(0, 0), (0, 1), (1, 0), (2, 0), (1, 1), (2, 1)]
+CHUNKS = [(0, 0), (1, 0), (0, 1), (1, 1), (2, 0), (2, 1)]
 PIECES = len(CHUNKS) * PASSES
 UNITS = len(CHUNKS) * B
 AHEAD = 4

from contextlib import ExitStack
import math

import concourse.mybir as mybir
from concourse.masks import make_identity

F32 = mybir.dt.float32
BF16 = mybir.dt.bfloat16
U32 = mybir.dt.uint32
U8 = mybir.dt.uint8
FP8X4 = mybir.dt.float8_e4m3fn_x4
ALU = mybir.AluOpType
ACT = mybir.ActivationFunctionType

P = 128
PACK = 4
B = 2
S = 512
H = 1024
HD = 128
EPS = 1e-7
PASSES = H // (P * PACK)
TOK_TILES = S // P
N_TILES = B * TOK_TILES
ROUNDS = B * PASSES
BANK = 512
CHUNK = BANK
CHUNK_HEADS = CHUNK // HD
K_TILES = H // P
CHUNKS = [(0, 0), (1, 0), (0, 1), (1, 1), (2, 0), (2, 1)]
PIECES = len(CHUNKS) * PASSES
UNITS = len(CHUNKS) * B
AHEAD = 4

FLOPS = 2 * B * S * H * 3 * H


def tile_disentangledattention_pa_kernel(
    tc, x, pos_emb, emb_ln_g, emb_ln_b, Wq, Wk, Wv, q_bias, v_bias, out_0, out_1, out_2
):
    nc = tc.nc
    weights = [Wq, Wk, Wv]
    outs = [out_0, out_1, out_2]
    inv_sqrt_hd = 1.0 / math.sqrt(HD)

    with ExitStack() as ctx:
        keep = ctx.enter_context(tc.tile_pool(name="keep", bufs=1))
        tokens = ctx.enter_context(tc.tile_pool(name="tokens", bufs=N_TILES))
        stats = ctx.enter_context(tc.tile_pool(name="stats", bufs=4))
        work = ctx.enter_context(tc.tile_pool(name="work", bufs=2))
        pieces = ctx.enter_context(tc.tile_pool(name="pieces", bufs=4))
        stores = ctx.enter_context(tc.tile_pool(name="stores", bufs=4))
        psum = ctx.enter_context(tc.psum_pool(name="psum", bufs=8))
        ctx.enter_context(tc.manual_schedule())

        ident_bf16 = keep.tile([P, P], BF16)
        make_identity(nc, ident_bf16[:])
        ident_f32 = keep.tile([P, P], F32)
        make_identity(nc, ident_f32[:])
        minus_half = keep.tile([P, 1], F32)
        nc.gpsimd.memset(minus_half[:], -0.5)

        bias_rows = keep.tile([P, H], BF16)
        nc.vector.memset(bias_rows[:].bitcast(U32), 0)
        for i, vec in enumerate((q_bias, v_bias)):
            nc.scalar.dma_start(out=bias_rows[i : i + 1, :], in_=vec.rearrange("(r h) -> r h", r=1))

        x_sb = keep.tile([P, B, TOK_TILES, H], BF16)
        pos_sb = keep.tile([P, TOK_TILES, H], BF16)
        pos_view = pos_emb.rearrange("(p j) h -> p j h", j=TOK_TILES)
        x_views = [x[b].rearrange("(p j) h -> p j h", j=TOK_TILES) for b in range(B)]
        for j in range(TOK_TILES):
            for cols in (slice(0, BANK), slice(BANK, H)) if j == 0 else (slice(0, H),):
                nc.sync.dma_start(out=pos_sb[:, j, cols], in_=pos_view[:, j, cols])
                nc.sync.dma_start(out=x_sb[:, 0, j, cols], in_=x_views[0][:, j, cols])
        for js in (slice(0, 2), slice(2, 4)):
            nc.sync.dma_start(out=x_sb[:, 1, js, :], in_=x_views[1][:, js, :])
        w_raw = [keep.tile([P, PASSES, PACK, H], BF16, name="w_raw%d" % m) for m in range(3)]
        for m in range(3):
            w_view = weights[m].rearrange("(c p t) n -> c p t n", c=PASSES, t=PACK)
            for c in range(PASSES):
                nc.sync.dma_start(out=w_raw[m][:, c, :, :], in_=w_view[c])
        gb_bf16 = []
        for i, vec in enumerate((emb_ln_g, emb_ln_b)):
            vec_cols = keep.tile([P, PASSES, PACK], BF16, name="vec_cols%d" % i)
            nc.scalar.dma_start(
                out=vec_cols[:], in_=vec.rearrange("(c p t) -> p c t", c=PASSES, t=PACK)
            )
            gb_bf16.append(vec_cols)

        h_codes = keep.tile([P, ROUNDS, S], U32, align_bytes=64)
        h_scales = keep.tile([P, ROUNDS, S], U8, align_bytes=64)
        w_codes = keep.tile([P, PIECES, CHUNK], U32, align_bytes=64)
        w_scales = keep.tile([P, PIECES, CHUNK], U8, align_bytes=64)

        def regroup(engine_copy, grouped, planes):
            engine_copy(
                out=grouped.rearrange("p (w i) t -> p w t i", i=4),
                in_=planes.rearrange("p t (w i) -> p w t i", i=4),
            )

        u_banks = {}
        moments = {}
        scale_shift = {}
        z_toks = {}

        def add_tokens(i):
            b, j = divmod(i, TOK_TILES)
            u_banks[i] = []
            for c in range(PASSES):
                cols = slice(c * BANK, (c + 1) * BANK)
                u_bank = psum.tile([P, BANK], F32, tag="bank")
                nc.tensor.matmul(
                    u_bank[:], lhsT=ident_bf16[:], rhs=x_sb[:, b, j, cols], start=True, stop=False
                )
                nc.tensor.matmul(
                    u_bank[:], lhsT=ident_bf16[:], rhs=pos_sb[:, j, cols], start=False, stop=True
                )
                u_banks[i].append(u_bank)
            moment = stats.tile([P, PASSES, 6], F32)
            moments[i] = moment

        def stats_half(i, c):
            nc.vector.bn_stats(out=moments[i][:, c, :], in_=u_banks[i][c][:])

        def finish_stats(i):
            mean_var = stats.tile([P, 2], F32)
            nc.vector.bn_aggr(out=mean_var[:], in_=moments[i][:].rearrange("p c s -> p (c s)"))
            var_eps = stats.tile([P, 1], F32)
            nc.gpsimd.tensor_scalar(
                out=var_eps[:], in0=mean_var[:, 1:2], scalar1=1.0, scalar2=EPS,
                op0=ALU.mult, op1=ALU.add,
            )
            rstd = stats.tile([P, 1], F32)
            nc.gpsimd.tensor_tensor(out=rstd[:], in0=var_eps[:], in1=minus_half[:], op=ALU.pow)
            shift = stats.tile([P, 1], F32)
            nc.gpsimd.tensor_scalar(
                out=shift[:], in0=mean_var[:, 0:1], scalar1=rstd[:], scalar2=-1.0,
                op0=ALU.mult, op1=ALU.mult,
            )
            scale_shift[i] = (rstd, shift)

        def normalise(i):
            rstd, shift = scale_shift[i]
            z_tok = tokens.tile([P, H], F32)
            for c in range(PASSES):
                nc.scalar.activation(
                    out=z_tok[:, c * BANK : (c + 1) * BANK].rearrange("p (t m) -> p t m", t=PACK),
                    in_=u_banks[i][c][:].rearrange("p (m t) -> p t m", t=PACK),
                    func=ACT.Identity, scale=rstd[:], bias=shift[:],
                )
            z_toks[i] = z_tok

        bias_all = keep.tile([P, 2, H], F32)

        def spread_bias():
            for i, factor in enumerate((inv_sqrt_hd, 1.0)):
                for half in range(PASSES):
                    cols = slice(half * BANK, (half + 1) * BANK)
                    bias_bank = psum.tile([P, BANK], F32, tag="bank")
                    nc.tensor.matmul(
                        bias_bank[:], lhsT=ident_bf16[:, i : i + 1].to_broadcast([P, P]),
                        rhs=bias_rows[:, cols], start=True, stop=True,
                    )
                    nc.scalar.activation(
                        out=bias_all[:, i, cols], in_=bias_bank[:], func=ACT.Identity, scale=factor
                    )

        add_tokens(0)
        for i in range(N_TILES + 1):
            if i + 1 < N_TILES:
                add_tokens(i + 1)
            if i == 0:
                spread_bias()
            if i < N_TILES:
                stats_half(i, 0)
            if i >= 1:
                finish_stats(i - 1)
            if i < N_TILES:
                stats_half(i, 1)
            if i >= 1:
                normalise(i - 1)

        gain_bias = keep.tile([P, 2 * K_TILES], F32)
        for i in range(2):
            nc.vector.tensor_copy(
                out=gain_bias[:, i * K_TILES : (i + 1) * K_TILES],
                in_=gb_bf16[i][:].rearrange("p c t -> p (c t)"),
            )

        zT_banks = {}
        h_planes = {}
        h_grouped = {}

        def transpose_round(r):
            b, c = divmod(r, PASSES)
            zT_banks[r] = []
            for t in range(PACK):
                kt = c * PACK + t
                zT_bank = psum.tile([P, S], F32, tag="bank")
                for j in range(TOK_TILES):
                    nc.tensor.transpose(
                        zT_bank[:, j * P : (j + 1) * P],
                        z_toks[b * TOK_TILES + j][:, kt * P : (kt + 1) * P],
                        ident_f32[:],
                    )
                zT_banks[r].append(zT_bank)

        def scale_round(r):
            c = r % PASSES
            planes = work.tile([P, PACK, S], BF16)
            for t in range(PACK):
                kt = c * PACK + t
                gain = gain_bias[:, kt : kt + 1]
                bias = gain_bias[:, K_TILES + kt : K_TILES + kt + 1]
                if r == 0:
                    nc.vector.tensor_scalar(
                        out=planes[:, t, :], in0=zT_banks[r][t][:], scalar1=gain, scalar2=bias,
                        op0=ALU.mult, op1=ALU.add,
                    )
                else:
                    nc.scalar.activation(
                        out=planes[:, t, :], in_=zT_banks[r][t][:], func=ACT.Identity,
                        scale=gain, bias=bias,
                    )
            h_planes[r] = planes

        def regroup_round(r):
            grouped = work.tile([P, S, PACK], BF16, align_bytes=64)
            regroup(nc.vector.tensor_copy, grouped[:], h_planes[r][:])
            h_grouped[r] = grouped

        def quantise_round(r):
            nc.vector.quantize_mx(
                out=h_codes[:, r, :].bitcast(FP8X4),
                scales=h_scales[:, r, :],
                in_=h_grouped[r][:].rearrange("p w t -> p (w t)"),
            )

        w_grouped = {}

        def regroup_piece(piece, engine_copy):
            (m, half), c = CHUNKS[piece // PASSES], piece % PASSES
            grouped_w = pieces.tile([P, CHUNK, PACK], BF16, align_bytes=64)
            regroup(engine_copy, grouped_w[:], w_raw[m][:, c, :, half * CHUNK : (half + 1) * CHUNK])
            w_grouped[piece] = grouped_w

        def quantise_piece(piece):
            nc.vector.quantize_mx(
                out=w_codes[:, piece, :].bitcast(FP8X4),
                scales=w_scales[:, piece, :],
                in_=w_grouped[piece][:].rearrange("p w t -> p (w t)"),
            )

        transpose_round(0)
        transpose_round(1)
        for r in range(ROUNDS):
            scale_round(r)
            if r + 2 < ROUNDS:
                transpose_round(r + 2)
            if r >= 1:
                if r - 1 < PASSES:
                    quantise_piece(r - 1)
                quantise_round(r - 1)
            if r < PASSES:
                regroup_piece(r, nc.vector.tensor_copy)
            regroup_round(r)
        quantise_round(ROUNDS - 1)
        for piece in range(PASSES, AHEAD):
            regroup_piece(piece, nc.scalar.copy)
        quantised = PASSES

        acc_banks = {}

        def multiply_unit(n):
            chunk, b = divmod(n, B)
            acc_banks[n] = []
            for j in range(TOK_TILES):
                acc = psum.tile([P, CHUNK], F32, tag="bank")
                for c in range(PASSES):
                    nc.tensor.matmul_mx(
                        out=acc[:],
                        lhsT=h_codes[:, b * PASSES + c, j * P : (j + 1) * P].bitcast(FP8X4),
                        lhsT_scale=h_scales[:, b * PASSES + c, j * P : (j + 1) * P],
                        rhs=w_codes[:, chunk * PASSES + c, :].bitcast(FP8X4),
                        rhs_scale=w_scales[:, chunk * PASSES + c, :],
                        start=(c == 0),
                        stop=(c == PASSES - 1),
                    )
                acc_banks[n].append(acc)

        def empty_unit(n):
            chunk, b = divmod(n, B)
            m, half = CHUNKS[chunk]
            cols = slice(half * CHUNK, (half + 1) * CHUNK)
            result = stores.tile([P, CHUNK_HEADS, TOK_TILES, HD], F32)
            for j in range(TOK_TILES):
                acc_heads = acc_banks[n][j][:].rearrange("p (n d) -> p n d", d=HD)
                if m == 0:
                    nc.vector.scalar_tensor_tensor(
                        out=result[:, :, j, :], in0=acc_heads, scalar=inv_sqrt_hd,
                        in1=bias_all[:, 0, cols].rearrange("p (n d) -> p n d", d=HD),
                        op0=ALU.mult, op1=ALU.add,
                    )
                elif m == 1:
                    nc.scalar.copy(out=result[:, :, j, :], in_=acc_heads)
                else:
                    nc.vector.tensor_tensor(
                        out=result[:, :, j, :], in0=acc_heads,
                        in1=bias_all[:, 1, cols].rearrange("p (n d) -> p n d", d=HD),
                        op=ALU.add,
                    )
            heads = slice(half * CHUNK_HEADS, (half + 1) * CHUNK_HEADS)
            nc.sync.dma_start(
                out=outs[m][b, heads].rearrange("n (p j) d -> p n (j d)", j=TOK_TILES),
                in_=result[:].rearrange("p n j d -> p n (j d)"),
            )

        multiply_unit(0)
        for n in range(UNITS):
            if n + 1 < UNITS:
                multiply_unit(n + 1)
            if n + AHEAD < PIECES:
                unit_of_k = CHUNKS[n // B][0] == 1
                regroup_piece(n + AHEAD, nc.vector.tensor_copy if unit_of_k else nc.scalar.copy)
            empty_unit(n)
            for piece in range(quantised, min(n + AHEAD, PIECES)):
                quantise_piece(piece)
            quantised = min(n + AHEAD, PIECES)
